import numpy as np
import ml_dtypes


def mxq(x, axis, fmt="e4m3"):
    dtype, down = {"e4m3": (ml_dtypes.float8_e4m3fn, 7), "e5m2": (ml_dtypes.float8_e5m2, 14)}[fmt]
    v = np.moveaxis(np.asarray(x, np.float32).astype(ml_dtypes.bfloat16).astype(np.float64), axis, -1)
    blocks = v.reshape(v.shape[:-1] + (-1, 32))
    amax = np.abs(blocks).max(-1, keepdims=True)
    byte = np.maximum(np.where(amax > 0, np.frexp(amax)[1] - 1 + 127, 0) - down, 1)
    scale = np.exp2(byte - 127.0)
    codes = (blocks / scale).astype(np.float32).astype(dtype).astype(np.float64)
    return np.moveaxis((codes * scale).reshape(v.shape), -1, axis)


WIDE = False


def mx_kscale(k):
    if not WIDE:
        return np.ones(k)
    levels = np.array([10, -10, 5, -5, 0])
    a = np.random.permutation(np.resize(levels, k // 512 * 4)).reshape(k // 512, 4)
    idx = np.arange(k)
    return np.exp2(a[idx // 512, idx % 128 // 32])


BF16 = ml_dtypes.bfloat16


def bf(x):
    return np.asarray(x, np.float32).astype(BF16)


def f64(x):
    return np.asarray(x).astype(np.float64)


BATCH, SIZE_IN, SIZE_OUT, STEPS = 256, 1024, 512, 8


def _build_mask(size_in, size_out, steps):
    inp_el_counts = size_in // steps
    rows = np.arange(size_out)
    count = rows % inp_el_counts
    cols = np.arange(steps)[None, :] * inp_el_counts + count[:, None]
    mask = np.zeros((size_out, size_in), dtype=np.float32)
    mask[rows[:, None], cols] = 1.0
    return mask


def setup_inputs():
    s = mx_kscale(SIZE_IN)
    bound = np.sqrt(3.0 / STEPS)
    return {"x": bf(np.random.standard_normal((BATCH, SIZE_IN)) * s),
            "weights": bf(np.random.uniform(-bound, bound, (SIZE_OUT, SIZE_IN)) / s[None, :]),
            "bias": bf(np.random.uniform(-0.5, 0.5, SIZE_OUT)),
            "mask": bf(_build_mask(SIZE_IN, SIZE_OUT, STEPS))}


def reference(x, weights, bias, mask):
    w = f64(weights) * f64(mask)
    return (mxq(f64(x), 1, "e4m3") @ mxq(w, 1, "e4m3").T) + f64(bias)

@@ -1,0 +1,112 @@
+from contextlib import ExitStack
+
+import concourse.mybir as mybir
+from concourse.masks import make_identity
+
+F32 = mybir.dt.float32
+BF16 = mybir.dt.bfloat16
+U32 = mybir.dt.uint32
+U8 = mybir.dt.uint8
+FP8X4 = mybir.dt.float8_e4m3fn_x4
+
+BATCH, SIZE_IN, SIZE_OUT = 256, 1024, 512
+FLOPS = 2 * BATCH * SIZE_IN * SIZE_OUT
+
+P = 128
+K_PASS = 4 * P
+PASSES = SIZE_IN // K_PASS
+PAIRS = 2
+X_TILES = BATCH // P
+W_TILES = SIZE_OUT // P
+
+
+def quantise_rows(nc, flip_banks, stage, identity, rows, codes, scales):
+    words = rows.bitcast(F32)
+    flipped = flip_banks.tile([P, PASSES, PAIRS, P], F32)
+    for g in range(PASSES):
+        for u in range(PAIRS):
+            block = PAIRS * g + u
+            nc.tensor.transpose(flipped[:, g, u, :], words[:, block * P : (block + 1) * P], identity)
+    grouped = stage.tile([P, SIZE_IN], BF16, align_bytes=64)
+    nc.scalar.copy(
+        out=grouped[:].bitcast(F32).rearrange("p (g r u) -> p g r u", g=PASSES, u=PAIRS),
+        in_=flipped[:].rearrange("p g u r -> p g r u"),
+    )
+    nc.vector.quantize_mx(out=codes.bitcast(FP8X4), scales=scales, in_=grouped[:])
+
+
+def tile_sparselayer_s_kernel(tc, x, weights, bias, mask, out):
+    nc = tc.nc
+    with ExitStack() as ctx:
+        keep = ctx.enter_context(tc.tile_pool(name="keep", bufs=1))
+        stage = ctx.enter_context(tc.tile_pool(name="stage", bufs=3))
+        flip_banks = ctx.enter_context(tc.psum_pool(name="flip_banks", bufs=3))
+        bias_banks = ctx.enter_context(tc.psum_pool(name="bias_banks", bufs=1))
+        sum_banks = ctx.enter_context(tc.psum_pool(name="sum_banks", bufs=4))
+
+        x_rows = keep.tile([P, X_TILES, SIZE_IN], BF16)
+        w_rows = keep.tile([P, W_TILES, SIZE_IN], BF16)
+        m_rows = keep.tile([P, W_TILES, SIZE_IN], BF16)
+        for t in range(X_TILES):
+            nc.sync.dma_start(out=x_rows[:, t, :], in_=x[t * P : (t + 1) * P, :])
+        for j in range(W_TILES):
+            nc.sync.dma_start(out=w_rows[:, j, :], in_=weights[j * P : (j + 1) * P, :])
+            nc.sync.dma_start(out=m_rows[:, j, :], in_=mask[j * P : (j + 1) * P, :])
+
+        identity = keep.tile([P, P], F32)
+        make_identity(nc, identity[:])
+
+        bias_rows = keep.tile([P, SIZE_OUT], BF16)
+        nc.vector.memset(bias_rows[:], 0.0)
+        nc.scalar.dma_start(out=bias_rows[0:1, :], in_=bias.rearrange("(o n) -> o n", o=1))
+        ones = keep.tile([P, P], BF16)
+        nc.vector.memset(ones[:], 1.0)
+        bias_bank = bias_banks.tile([P, SIZE_OUT], F32)
+        nc.tensor.matmul(bias_bank[:], lhsT=ones[:], rhs=bias_rows[:], start=True, stop=True)
+        bias_all = keep.tile([P, SIZE_OUT], F32)
+        nc.scalar.copy(out=bias_all[:], in_=bias_bank[:])
+
+        x_codes = keep.tile([P, X_TILES, PASSES, P], U32, align_bytes=64)
+        x_scales = keep.tile([P, X_TILES, PASSES, P], U8, align_bytes=64)
+        w_codes = keep.tile([P, W_TILES, PASSES, P], U32, align_bytes=64)
+        w_scales = keep.tile([P, W_TILES, PASSES, P], U8, align_bytes=64)
+        masked = keep.tile([P, W_TILES, SIZE_IN], BF16)
+        result = keep.tile([P, X_TILES, SIZE_OUT], F32)
+        out_view = out.rearrange("(t p) n -> p t n", p=P)
+
+        for t in range(X_TILES):
+            quantise_rows(
+                nc, flip_banks, stage, identity[:], x_rows[:, t, :],
+                x_codes[:, t, :, :].rearrange("p g r -> p (g r)"),
+                x_scales[:, t, :, :].rearrange("p g r -> p (g r)"),
+            )
+
+        for j in range(W_TILES):
+            nc.vector.tensor_tensor(
+                out=masked[:, j, :], in0=w_rows[:, j, :], in1=m_rows[:, j, :], op=mybir.AluOpType.mult
+            )
+            quantise_rows(
+                nc, flip_banks, stage, identity[:], masked[:, j, :],
+                w_codes[:, j, :, :].rearrange("p g r -> p (g r)"),
+                w_scales[:, j, :, :].rearrange("p g r -> p (g r)"),
+            )
+            sums = sum_banks.tile([P, X_TILES, P], F32)
+            for t in range(X_TILES):
+                for g in range(PASSES):
+                    nc.tensor.matmul_mx(
+                        out=sums[:, t, :],
+                        lhsT=x_codes[:, t, g, :].bitcast(FP8X4),
+                        lhsT_scale=x_scales[:, t, g, :],
+                        rhs=w_codes[:, j, g, :].bitcast(FP8X4),
+                        rhs_scale=w_scales[:, j, g, :],
+                        start=(g == 0),
+                        stop=(g == PASSES - 1),
+                    )
+            n_cols = slice(j * P, (j + 1) * P)
+            nc.vector.tensor_tensor(
+                out=result[:, :, n_cols],
+                in0=sums[:],
+                in1=bias_all[:, n_cols].unsqueeze(1).to_broadcast([P, X_TILES, P]),
+                op=mybir.AluOpType.add,
+            )
+            nc.sync.dma_start(out=out_view[:, :, n_cols], in_=result[:, :, n_cols])

@@ -20,76 +20,72 @@ X_TILES = BATCH // P
 W_TILES = SIZE_OUT // P
 
 
-def quantise_rows(nc, flip_banks, stage, identity, rows, codes, scales):
-    words = rows.bitcast(F32)
-    flipped = flip_banks.tile([P, PASSES, PAIRS, P], F32)
-    for g in range(PASSES):
-        for u in range(PAIRS):
-            block = PAIRS * g + u
-            nc.tensor.transpose(flipped[:, g, u, :], words[:, block * P : (block + 1) * P], identity)
-    grouped = stage.tile([P, SIZE_IN], BF16, align_bytes=64)
-    nc.scalar.copy(
-        out=grouped[:].bitcast(F32).rearrange("p (g r u) -> p g r u", g=PASSES, u=PAIRS),
-        in_=flipped[:].rearrange("p g u r -> p g r u"),
-    )
-    nc.vector.quantize_mx(out=codes.bitcast(FP8X4), scales=scales, in_=grouped[:])
-
-
 def tile_sparselayer_s_kernel(tc, x, weights, bias, mask, out):
     nc = tc.nc
     with ExitStack() as ctx:
         keep = ctx.enter_context(tc.tile_pool(name="keep", bufs=1))
-        stage = ctx.enter_context(tc.tile_pool(name="stage", bufs=3))
-        flip_banks = ctx.enter_context(tc.psum_pool(name="flip_banks", bufs=3))
-        bias_banks = ctx.enter_context(tc.psum_pool(name="bias_banks", bufs=1))
+        stage = ctx.enter_context(tc.tile_pool(name="stage", bufs=6))
+        flip_banks = ctx.enter_context(tc.psum_pool(name="flip_banks", bufs=4))
         sum_banks = ctx.enter_context(tc.psum_pool(name="sum_banks", bufs=4))
+        ctx.enter_context(tc.manual_schedule())
 
         x_rows = keep.tile([P, X_TILES, SIZE_IN], BF16)
         w_rows = keep.tile([P, W_TILES, SIZE_IN], BF16)
         m_rows = keep.tile([P, W_TILES, SIZE_IN], BF16)
+        bias_rows = keep.tile([P, SIZE_OUT], BF16)
+        nc.gpsimd.memset(bias_rows[:], 0.0)
         for t in range(X_TILES):
             nc.sync.dma_start(out=x_rows[:, t, :], in_=x[t * P : (t + 1) * P, :])
+        nc.sync.dma_start(out=bias_rows[0:1, :], in_=bias.rearrange("(o n) -> o n", o=1))
         for j in range(W_TILES):
             nc.sync.dma_start(out=w_rows[:, j, :], in_=weights[j * P : (j + 1) * P, :])
             nc.sync.dma_start(out=m_rows[:, j, :], in_=mask[j * P : (j + 1) * P, :])
 
         identity = keep.tile([P, P], F32)
         make_identity(nc, identity[:])
-
-        bias_rows = keep.tile([P, SIZE_OUT], BF16)
-        nc.vector.memset(bias_rows[:], 0.0)
-        nc.scalar.dma_start(out=bias_rows[0:1, :], in_=bias.rearrange("(o n) -> o n", o=1))
         ones = keep.tile([P, P], BF16)
         nc.vector.memset(ones[:], 1.0)
-        bias_bank = bias_banks.tile([P, SIZE_OUT], F32)
-        nc.tensor.matmul(bias_bank[:], lhsT=ones[:], rhs=bias_rows[:], start=True, stop=True)
-        bias_all = keep.tile([P, SIZE_OUT], F32)
-        nc.scalar.copy(out=bias_all[:], in_=bias_bank[:])
 
         x_codes = keep.tile([P, X_TILES, PASSES, P], U32, align_bytes=64)
         x_scales = keep.tile([P, X_TILES, PASSES, P], U8, align_bytes=64)
         w_codes = keep.tile([P, W_TILES, PASSES, P], U32, align_bytes=64)
         w_scales = keep.tile([P, W_TILES, PASSES, P], U8, align_bytes=64)
         masked = keep.tile([P, W_TILES, SIZE_IN], BF16)
+        bias_all = keep.tile([P, SIZE_OUT], F32)
         result = keep.tile([P, X_TILES, SIZE_OUT], F32)
         out_view = out.rearrange("(t p) n -> p t n", p=P)
 
-        for t in range(X_TILES):
-            quantise_rows(
-                nc, flip_banks, stage, identity[:], x_rows[:, t, :],
-                x_codes[:, t, :, :].rearrange("p g r -> p (g r)"),
-                x_scales[:, t, :, :].rearrange("p g r -> p (g r)"),
-            )
+        def flip(rows):
+            words = rows.bitcast(F32)
+            grouped_passes = []
+            for g in range(PASSES):
+                flipped = flip_banks.tile([P, PAIRS, P], F32, tag="flipped")
+                for u in range(PAIRS):
+                    block = PAIRS * g + u
+                    nc.tensor.transpose(flipped[:, u, :], words[:, block * P : (block + 1) * P], identity[:])
+                grouped = stage.tile([P, K_PASS], BF16, align_bytes=64)
+                nc.scalar.copy(
+                    out=grouped[:].bitcast(F32).rearrange("p (r u) -> p r u", u=PAIRS),
+                    in_=flipped[:].rearrange("p u r -> p r u"),
+                )
+                grouped_passes.append(grouped)
+            return grouped_passes
 
-        for j in range(W_TILES):
-            nc.vector.tensor_tensor(
-                out=masked[:, j, :], in0=w_rows[:, j, :], in1=m_rows[:, j, :], op=mybir.AluOpType.mult
-            )
-            quantise_rows(
-                nc, flip_banks, stage, identity[:], masked[:, j, :],
-                w_codes[:, j, :, :].rearrange("p g r -> p (g r)"),
-                w_scales[:, j, :, :].rearrange("p g r -> p (g r)"),
-            )
+        def quantise(grouped_passes, codes, scales):
+            for g in range(PASSES):
+                nc.vector.quantize_mx(
+                    out=codes[:, g, :].bitcast(FP8X4), scales=scales[:, g, :], in_=grouped_passes[g][:]
+                )
+
+        def apply_mask(j):
+            for g in range(PASSES):
+                k_cols = slice(g * K_PASS, (g + 1) * K_PASS)
+                nc.vector.tensor_tensor(
+                    out=masked[:, j, k_cols], in0=w_rows[:, j, k_cols], in1=m_rows[:, j, k_cols],
+                    op=mybir.AluOpType.mult,
+                )
+
+        def multiply(j):
             sums = sum_banks.tile([P, X_TILES, P], F32)
             for t in range(X_TILES):
                 for g in range(PASSES):
@@ -102,6 +98,9 @@ def tile_sparselayer_s_kernel(tc, x, weights, bias, mask, out):
                         start=(g == 0),
                         stop=(g == PASSES - 1),
                     )
+            return sums
+
+        def add_bias_and_store(j, sums):
             n_cols = slice(j * P, (j + 1) * P)
             nc.vector.tensor_tensor(
                 out=result[:, :, n_cols],
@@ -110,3 +109,26 @@ def tile_sparselayer_s_kernel(tc, x, weights, bias, mask, out):
                 op=mybir.AluOpType.add,
             )
             nc.sync.dma_start(out=out_view[:, :, n_cols], in_=result[:, :, n_cols])
+
+        x_grouped = [flip(x_rows[:, t, :]) for t in range(X_TILES)]
+        quantise(x_grouped[0], x_codes[:, 0, :, :], x_scales[:, 0, :, :])
+        apply_mask(0)
+        quantise(x_grouped[1], x_codes[:, 1, :, :], x_scales[:, 1, :, :])
+        apply_mask(1)
+
+        bias_bank = flip_banks.tile([P, SIZE_OUT], F32, tag="flipped")
+        nc.tensor.matmul(bias_bank[:], lhsT=ones[:], rhs=bias_rows[:], start=True, stop=True)
+        nc.scalar.copy(out=bias_all[:], in_=bias_bank[:])
+
+        sums = None
+        for j in range(W_TILES):
+            w_grouped = flip(masked[:, j, :])
+            if j > 0:
+                sums = multiply(j - 1)
+            quantise(w_grouped, w_codes[:, j, :, :], w_scales[:, j, :, :])
+            if j > 0:
+                add_bias_and_store(j - 1, sums)
+            if j + 2 < W_TILES:
+                apply_mask(j + 2)
+        sums = multiply(W_TILES - 1)
+        add_bias_and_store(W_TILES - 1, sums)

@@ -24,7 +24,6 @@ def tile_sparselayer_s_kernel(tc, x, weights, bias, mask, out):
     nc = tc.nc
     with ExitStack() as ctx:
         keep = ctx.enter_context(tc.tile_pool(name="keep", bufs=1))
-        stage = ctx.enter_context(tc.tile_pool(name="stage", bufs=6))
         flip_banks = ctx.enter_context(tc.psum_pool(name="flip_banks", bufs=4))
         sum_banks = ctx.enter_context(tc.psum_pool(name="sum_banks", bufs=4))
         ctx.enter_context(tc.manual_schedule())
@@ -38,54 +37,70 @@ def tile_sparselayer_s_kernel(tc, x, weights, bias, mask, out):
             nc.sync.dma_start(out=x_rows[:, t, :], in_=x[t * P : (t + 1) * P, :])
         nc.sync.dma_start(out=bias_rows[0:1, :], in_=bias.rearrange("(o n) -> o n", o=1))
         for j in range(W_TILES):
-            nc.sync.dma_start(out=w_rows[:, j, :], in_=weights[j * P : (j + 1) * P, :])
-            nc.sync.dma_start(out=m_rows[:, j, :], in_=mask[j * P : (j + 1) * P, :])
+            n_rows = slice(j * P, (j + 1) * P)
+            nc.sync.dma_start(out=w_rows[:, j, :], in_=weights[n_rows, :])
+            if j < W_TILES - 1:
+                nc.sync.dma_start(out=m_rows[:, j, :], in_=mask[n_rows, :])
+            else:
+                for g in range(PASSES):
+                    k_cols = slice(g * K_PASS, (g + 1) * K_PASS)
+                    nc.sync.dma_start(out=m_rows[:, j, k_cols], in_=mask[n_rows, k_cols])
 
         identity = keep.tile([P, P], F32)
         make_identity(nc, identity[:])
         ones = keep.tile([P, P], BF16)
         nc.vector.memset(ones[:], 1.0)
 
+        masked = keep.tile([P, W_TILES, SIZE_IN], BF16)
+        x_grouped = keep.tile([P, X_TILES, PASSES, K_PASS], BF16, align_bytes=64)
+        w_grouped = keep.tile([P, W_TILES, PASSES, K_PASS], BF16, align_bytes=64)
         x_codes = keep.tile([P, X_TILES, PASSES, P], U32, align_bytes=64)
         x_scales = keep.tile([P, X_TILES, PASSES, P], U8, align_bytes=64)
         w_codes = keep.tile([P, W_TILES, PASSES, P], U32, align_bytes=64)
         w_scales = keep.tile([P, W_TILES, PASSES, P], U8, align_bytes=64)
-        masked = keep.tile([P, W_TILES, SIZE_IN], BF16)
         bias_all = keep.tile([P, SIZE_OUT], F32)
         result = keep.tile([P, X_TILES, SIZE_OUT], F32)
         out_view = out.rearrange("(t p) n -> p t n", p=P)
 
-        def flip(rows):
+        def flip(rows, grouped):
             words = rows.bitcast(F32)
-            grouped_passes = []
             for g in range(PASSES):
                 flipped = flip_banks.tile([P, PAIRS, P], F32, tag="flipped")
                 for u in range(PAIRS):
                     block = PAIRS * g + u
                     nc.tensor.transpose(flipped[:, u, :], words[:, block * P : (block + 1) * P], identity[:])
-                grouped = stage.tile([P, K_PASS], BF16, align_bytes=64)
                 nc.scalar.copy(
-                    out=grouped[:].bitcast(F32).rearrange("p (r u) -> p r u", u=PAIRS),
+                    out=grouped[:, g, :].bitcast(F32).rearrange("p (r u) -> p r u", u=PAIRS),
                     in_=flipped[:].rearrange("p u r -> p r u"),
                 )
-                grouped_passes.append(grouped)
-            return grouped_passes
 
-        def quantise(grouped_passes, codes, scales):
+        def quantise(grouped, codes, scales):
             for g in range(PASSES):
                 nc.vector.quantize_mx(
-                    out=codes[:, g, :].bitcast(FP8X4), scales=scales[:, g, :], in_=grouped_passes[g][:]
+                    out=codes[:, g, :].bitcast(FP8X4), scales=scales[:, g, :], in_=grouped[:, g, :]
                 )
 
-        def apply_mask(j):
+        for t in range(X_TILES):
+            flip(x_rows[:, t, :], x_grouped[:, t, :, :])
+        for t in range(X_TILES):
+            quantise(x_grouped[:, t, :, :], x_codes[:, t, :, :], x_scales[:, t, :, :])
+
+        bias_bank = flip_banks.tile([P, SIZE_OUT], F32, tag="flipped")
+        nc.tensor.matmul(bias_bank[:], lhsT=ones[:], rhs=bias_rows[:], start=True, stop=True)
+        nc.scalar.copy(out=bias_all[:], in_=bias_bank[:])
+
+        for j in range(W_TILES):
             for g in range(PASSES):
                 k_cols = slice(g * K_PASS, (g + 1) * K_PASS)
                 nc.vector.tensor_tensor(
                     out=masked[:, j, k_cols], in0=w_rows[:, j, k_cols], in1=m_rows[:, j, k_cols],
                     op=mybir.AluOpType.mult,
                 )
+            flip(masked[:, j, :], w_grouped[:, j, :, :])
+        for j in range(W_TILES):
+            quantise(w_grouped[:, j, :, :], w_codes[:, j, :, :], w_scales[:, j, :, :])
 
-        def multiply(j):
+        for j in range(W_TILES):
             sums = sum_banks.tile([P, X_TILES, P], F32)
             for t in range(X_TILES):
                 for g in range(PASSES):
@@ -98,9 +113,6 @@ def tile_sparselayer_s_kernel(tc, x, weights, bias, mask, out):
                         start=(g == 0),
                         stop=(g == PASSES - 1),
                     )
-            return sums
-
-        def add_bias_and_store(j, sums):
             n_cols = slice(j * P, (j + 1) * P)
             nc.vector.tensor_tensor(
                 out=result[:, :, n_cols],
@@ -109,26 +121,3 @@ def tile_sparselayer_s_kernel(tc, x, weights, bias, mask, out):
                 op=mybir.AluOpType.add,
             )
             nc.sync.dma_start(out=out_view[:, :, n_cols], in_=result[:, :, n_cols])
-
-        x_grouped = [flip(x_rows[:, t, :]) for t in range(X_TILES)]
-        quantise(x_grouped[0], x_codes[:, 0, :, :], x_scales[:, 0, :, :])
-        apply_mask(0)
-        quantise(x_grouped[1], x_codes[:, 1, :, :], x_scales[:, 1, :, :])
-        apply_mask(1)
-
-        bias_bank = flip_banks.tile([P, SIZE_OUT], F32, tag="flipped")
-        nc.tensor.matmul(bias_bank[:], lhsT=ones[:], rhs=bias_rows[:], start=True, stop=True)
-        nc.scalar.copy(out=bias_all[:], in_=bias_bank[:])
-
-        sums = None
-        for j in range(W_TILES):
-            w_grouped = flip(masked[:, j, :])
-            if j > 0:
-                sums = multiply(j - 1)
-            quantise(w_grouped, w_codes[:, j, :, :], w_scales[:, j, :, :])
-            if j > 0:
-                add_bias_and_store(j - 1, sums)
-            if j + 2 < W_TILES:
-                apply_mask(j + 2)
-        sums = multiply(W_TILES - 1)
-        add_bias_and_store(W_TILES - 1, sums)

@@ -18,6 +18,9 @@ PASSES = SIZE_IN // K_PASS
 PAIRS = 2
 X_TILES = BATCH // P
 W_TILES = SIZE_OUT // P
+HALF = W_TILES // 2
+EARLY = 1
+assert X_TILES == HALF
 
 
 def tile_sparselayer_s_kernel(tc, x, weights, bias, mask, out):
@@ -80,27 +83,15 @@ def tile_sparselayer_s_kernel(tc, x, weights, bias, mask, out):
                     out=codes[:, g, :].bitcast(FP8X4), scales=scales[:, g, :], in_=grouped[:, g, :]
                 )
 
-        for t in range(X_TILES):
-            flip(x_rows[:, t, :], x_grouped[:, t, :, :])
-        for t in range(X_TILES):
-            quantise(x_grouped[:, t, :, :], x_codes[:, t, :, :], x_scales[:, t, :, :])
-
-        bias_bank = flip_banks.tile([P, SIZE_OUT], F32, tag="flipped")
-        nc.tensor.matmul(bias_bank[:], lhsT=ones[:], rhs=bias_rows[:], start=True, stop=True)
-        nc.scalar.copy(out=bias_all[:], in_=bias_bank[:])
-
-        for j in range(W_TILES):
+        def apply_mask(j):
             for g in range(PASSES):
                 k_cols = slice(g * K_PASS, (g + 1) * K_PASS)
                 nc.vector.tensor_tensor(
                     out=masked[:, j, k_cols], in0=w_rows[:, j, k_cols], in1=m_rows[:, j, k_cols],
                     op=mybir.AluOpType.mult,
                 )
-            flip(masked[:, j, :], w_grouped[:, j, :, :])
-        for j in range(W_TILES):
-            quantise(w_grouped[:, j, :, :], w_codes[:, j, :, :], w_scales[:, j, :, :])
 
-        for j in range(W_TILES):
+        def multiply(j):
             sums = sum_banks.tile([P, X_TILES, P], F32)
             for t in range(X_TILES):
                 for g in range(PASSES):
@@ -113,6 +104,9 @@ def tile_sparselayer_s_kernel(tc, x, weights, bias, mask, out):
                         start=(g == 0),
                         stop=(g == PASSES - 1),
                     )
+            return sums
+
+        def add_bias_and_store(j, sums):
             n_cols = slice(j * P, (j + 1) * P)
             nc.vector.tensor_tensor(
                 out=result[:, :, n_cols],
@@ -121,3 +115,29 @@ def tile_sparselayer_s_kernel(tc, x, weights, bias, mask, out):
                 op=mybir.AluOpType.add,
             )
             nc.sync.dma_start(out=out_view[:, :, n_cols], in_=result[:, :, n_cols])
+
+        for t in range(X_TILES):
+            flip(x_rows[:, t, :], x_grouped[:, t, :, :])
+        for t in range(X_TILES):
+            quantise(x_grouped[:, t, :, :], x_codes[:, t, :, :], x_scales[:, t, :, :])
+            apply_mask(t)
+
+        bias_bank = flip_banks.tile([P, SIZE_OUT], F32, tag="flipped")
+        nc.tensor.matmul(bias_bank[:], lhsT=ones[:], rhs=bias_rows[:], start=True, stop=True)
+        nc.scalar.copy(out=bias_all[:], in_=bias_bank[:])
+
+        sums = {}
+        for j in range(HALF):
+            flip(masked[:, j, :], w_grouped[:, j, :, :])
+        for j in range(EARLY):
+            quantise(w_grouped[:, j, :, :], w_codes[:, j, :, :], w_scales[:, j, :, :])
+            sums[j] = multiply(j)
+        for j in range(HALF, W_TILES):
+            apply_mask(j)
+            flip(masked[:, j, :], w_grouped[:, j, :, :])
+
+        for j in range(EARLY, W_TILES):
+            quantise(w_grouped[:, j, :, :], w_codes[:, j, :, :], w_scales[:, j, :, :])
+            sums[j] = multiply(j)
+        for j in range(W_TILES):
+            add_bias_and_store(j, sums[j])

@@ -91,19 +91,22 @@ def tile_sparselayer_s_kernel(tc, x, weights, bias, mask, out):
                     op=mybir.AluOpType.mult,
                 )
 
+        def multiply_pass(out, j, t, g):
+            nc.tensor.matmul_mx(
+                out=out,
+                lhsT=x_codes[:, t, g, :].bitcast(FP8X4),
+                lhsT_scale=x_scales[:, t, g, :],
+                rhs=w_codes[:, j, g, :].bitcast(FP8X4),
+                rhs_scale=w_scales[:, j, g, :],
+                start=(g == 0),
+                stop=(g == PASSES - 1),
+            )
+
         def multiply(j):
             sums = sum_banks.tile([P, X_TILES, P], F32)
             for t in range(X_TILES):
                 for g in range(PASSES):
-                    nc.tensor.matmul_mx(
-                        out=sums[:, t, :],
-                        lhsT=x_codes[:, t, g, :].bitcast(FP8X4),
-                        lhsT_scale=x_scales[:, t, g, :],
-                        rhs=w_codes[:, j, g, :].bitcast(FP8X4),
-                        rhs_scale=w_scales[:, j, g, :],
-                        start=(g == 0),
-                        stop=(g == PASSES - 1),
-                    )
+                    multiply_pass(sums[:, t, :], j, t, g)
             return sums
 
         def add_bias_and_store(j, sums):
@@ -136,8 +139,25 @@ def tile_sparselayer_s_kernel(tc, x, weights, bias, mask, out):
             apply_mask(j)
             flip(masked[:, j, :], w_grouped[:, j, :, :])
 
-        for j in range(EARLY, W_TILES):
+        for j in range(EARLY, W_TILES - 1):
             quantise(w_grouped[:, j, :, :], w_codes[:, j, :, :], w_scales[:, j, :, :])
             sums[j] = multiply(j)
-        for j in range(W_TILES):
+            if j == EARLY:
+                add_bias_and_store(0, sums[0])
+
+        last = W_TILES - 1
+        halves = [sum_banks.tile([P, X_TILES, P], F32, name=f"half{t}", tag="sums") for t in range(X_TILES)]
+        for g in range(PASSES):
+            nc.vector.quantize_mx(
+                out=w_codes[:, last, g, :].bitcast(FP8X4), scales=w_scales[:, last, g, :], in_=w_grouped[:, last, g, :]
+            )
+            for t in range(X_TILES):
+                multiply_pass(halves[t][:, 0, :], last, t, g)
+        for j in range(EARLY, last):
             add_bias_and_store(j, sums[j])
+        n_cols = slice(last * P, W_TILES * P)
+        for t in range(X_TILES):
+            nc.vector.tensor_tensor(
+                out=result[:, t, n_cols], in0=halves[t][:, 0, :], in1=bias_all[:, n_cols], op=mybir.AluOpType.add
+            )
+        nc.sync.dma_start(out=out_view[:, :, n_cols], in_=result[:, :, n_cols])

@@ -18,9 +18,7 @@ PASSES = SIZE_IN // K_PASS
 PAIRS = 2
 X_TILES = BATCH // P
 W_TILES = SIZE_OUT // P
-HALF = W_TILES // 2
-EARLY = 1
-assert X_TILES == HALF
+HALVES = 2
 
 
 def tile_sparselayer_s_kernel(tc, x, weights, bias, mask, out):
@@ -36,8 +34,7 @@ def tile_sparselayer_s_kernel(tc, x, weights, bias, mask, out):
         m_rows = keep.tile([P, W_TILES, SIZE_IN], BF16)
         bias_rows = keep.tile([P, SIZE_OUT], BF16)
         nc.gpsimd.memset(bias_rows[:], 0.0)
-        for t in range(X_TILES):
-            nc.sync.dma_start(out=x_rows[:, t, :], in_=x[t * P : (t + 1) * P, :])
+        nc.sync.dma_start(out=x_rows[:], in_=x.rearrange("(p t) k -> p t k", t=X_TILES))
         nc.sync.dma_start(out=bias_rows[0:1, :], in_=bias.rearrange("(o n) -> o n", o=1))
         for j in range(W_TILES):
             n_rows = slice(j * P, (j + 1) * P)
@@ -63,19 +60,21 @@ def tile_sparselayer_s_kernel(tc, x, weights, bias, mask, out):
         w_scales = keep.tile([P, W_TILES, PASSES, P], U8, align_bytes=64)
         bias_all = keep.tile([P, SIZE_OUT], F32)
         result = keep.tile([P, X_TILES, SIZE_OUT], F32)
-        out_view = out.rearrange("(t p) n -> p t n", p=P)
+        out_view = out.rearrange("(p t) n -> p t n", t=X_TILES)
 
-        def flip(rows, grouped):
+        def flip(rows, grouped, last_parts=1):
             words = rows.bitcast(F32)
             for g in range(PASSES):
                 flipped = flip_banks.tile([P, PAIRS, P], F32, tag="flipped")
                 for u in range(PAIRS):
                     block = PAIRS * g + u
                     nc.tensor.transpose(flipped[:, u, :], words[:, block * P : (block + 1) * P], identity[:])
-                nc.scalar.copy(
-                    out=grouped[:, g, :].bitcast(F32).rearrange("p (r u) -> p r u", u=PAIRS),
-                    in_=flipped[:].rearrange("p u r -> p r u"),
-                )
+                words_out = grouped[:, g, :].bitcast(F32).rearrange("p (r u) -> p r u", u=PAIRS)
+                words_in = flipped[:].rearrange("p u r -> p r u")
+                parts = last_parts if g == PASSES - 1 else 1
+                for h in range(parts):
+                    r = slice(h * P // parts, (h + 1) * P // parts)
+                    nc.scalar.copy(out=words_out[:, r, :], in_=words_in[:, r, :])
 
         def quantise(grouped, codes, scales):
             for g in range(PASSES):
@@ -84,8 +83,10 @@ def tile_sparselayer_s_kernel(tc, x, weights, bias, mask, out):
                 )
 
         def apply_mask(j):
-            for g in range(PASSES):
-                k_cols = slice(g * K_PASS, (g + 1) * K_PASS)
+            block = K_PASS // PAIRS
+            bounds = [0, K_PASS, SIZE_IN] if j < W_TILES - 1 else [0, K_PASS, K_PASS + block, SIZE_IN]
+            for first, end in zip(bounds[:-1], bounds[1:]):
+                k_cols = slice(first, end)
                 nc.vector.tensor_tensor(
                     out=masked[:, j, k_cols], in0=w_rows[:, j, k_cols], in1=m_rows[:, j, k_cols],
                     op=mybir.AluOpType.mult,
@@ -121,39 +122,47 @@ def tile_sparselayer_s_kernel(tc, x, weights, bias, mask, out):
 
         for t in range(X_TILES):
             flip(x_rows[:, t, :], x_grouped[:, t, :, :])
+        apply_mask(0)
         for t in range(X_TILES):
             quantise(x_grouped[:, t, :, :], x_codes[:, t, :, :], x_scales[:, t, :, :])
-            apply_mask(t)
+        flip(masked[:, 0, :], w_grouped[:, 0, :, :])
 
         bias_bank = flip_banks.tile([P, SIZE_OUT], F32, tag="flipped")
         nc.tensor.matmul(bias_bank[:], lhsT=ones[:], rhs=bias_rows[:], start=True, stop=True)
         nc.scalar.copy(out=bias_all[:], in_=bias_bank[:])
 
+        apply_mask(1)
+        flip(masked[:, 1, :], w_grouped[:, 1, :, :])
+
         sums = {}
-        for j in range(HALF):
-            flip(masked[:, j, :], w_grouped[:, j, :, :])
-        for j in range(EARLY):
-            quantise(w_grouped[:, j, :, :], w_codes[:, j, :, :], w_scales[:, j, :, :])
-            sums[j] = multiply(j)
-        for j in range(HALF, W_TILES):
+        quantise(w_grouped[:, 0, :, :], w_codes[:, 0, :, :], w_scales[:, 0, :, :])
+        sums[0] = multiply(0)
+        last = W_TILES - 1
+        for j in range(2, last):
             apply_mask(j)
             flip(masked[:, j, :], w_grouped[:, j, :, :])
+        apply_mask(last)
+        flip(masked[:, last, :], w_grouped[:, last, :, :], last_parts=HALVES)
+        add_bias_and_store(0, sums[0])
 
-        for j in range(EARLY, W_TILES - 1):
+        for j in range(1, last):
             quantise(w_grouped[:, j, :, :], w_codes[:, j, :, :], w_scales[:, j, :, :])
             sums[j] = multiply(j)
-            if j == EARLY:
-                add_bias_and_store(0, sums[0])
 
-        last = W_TILES - 1
         halves = [sum_banks.tile([P, X_TILES, P], F32, name=f"half{t}", tag="sums") for t in range(X_TILES)]
         for g in range(PASSES):
-            nc.vector.quantize_mx(
-                out=w_codes[:, last, g, :].bitcast(FP8X4), scales=w_scales[:, last, g, :], in_=w_grouped[:, last, g, :]
-            )
+            parts = HALVES if g == PASSES - 1 else 1
+            for h in range(parts):
+                r = slice(h * P // parts, (h + 1) * P // parts)
+                k_values = slice(h * K_PASS // parts, (h + 1) * K_PASS // parts)
+                nc.vector.quantize_mx(
+                    out=w_codes[:, last, g, r].bitcast(FP8X4),
+                    scales=w_scales[:, last, g, r],
+                    in_=w_grouped[:, last, g, k_values],
+                )
             for t in range(X_TILES):
                 multiply_pass(halves[t][:, 0, :], last, t, g)
-        for j in range(EARLY, last):
+        for j in range(1, last):
             add_bias_and_store(j, sums[j])
         n_cols = slice(last * P, W_TILES * P)
         for t in range(X_TILES):

from contextlib import ExitStack

import concourse.mybir as mybir
from concourse.masks import make_identity

F32 = mybir.dt.float32
BF16 = mybir.dt.bfloat16
U32 = mybir.dt.uint32
U8 = mybir.dt.uint8
FP8X4 = mybir.dt.float8_e4m3fn_x4

BATCH, SIZE_IN, SIZE_OUT = 256, 1024, 512
FLOPS = 2 * BATCH * SIZE_IN * SIZE_OUT

P = 128
K_PASS = 4 * P
PASSES = SIZE_IN // K_PASS
PAIRS = 2
X_TILES = BATCH // P
W_TILES = SIZE_OUT // P
HALVES = 2


def tile_sparselayer_s_kernel(tc, x, weights, bias, mask, out):
    nc = tc.nc
    with ExitStack() as ctx:
        keep = ctx.enter_context(tc.tile_pool(name="keep", bufs=1))
        flip_banks = ctx.enter_context(tc.psum_pool(name="flip_banks", bufs=4))
        sum_banks = ctx.enter_context(tc.psum_pool(name="sum_banks", bufs=4))
        ctx.enter_context(tc.manual_schedule())

        x_rows = keep.tile([P, X_TILES, SIZE_IN], BF16)
        w_rows = keep.tile([P, W_TILES, SIZE_IN], BF16)
        m_rows = keep.tile([P, W_TILES, SIZE_IN], BF16)
        bias_rows = keep.tile([P, SIZE_OUT], BF16)
        nc.gpsimd.memset(bias_rows[:], 0.0)
        nc.sync.dma_start(out=x_rows[:], in_=x.rearrange("(p t) k -> p t k", t=X_TILES))
        nc.sync.dma_start(out=bias_rows[0:1, :], in_=bias.rearrange("(o n) -> o n", o=1))
        for j in range(W_TILES):
            n_rows = slice(j * P, (j + 1) * P)
            nc.sync.dma_start(out=w_rows[:, j, :], in_=weights[n_rows, :])
            if j < W_TILES - 1:
                nc.sync.dma_start(out=m_rows[:, j, :], in_=mask[n_rows, :])
            else:
                for g in range(PASSES):
                    k_cols = slice(g * K_PASS, (g + 1) * K_PASS)
                    nc.sync.dma_start(out=m_rows[:, j, k_cols], in_=mask[n_rows, k_cols])

        identity = keep.tile([P, P], F32)
        make_identity(nc, identity[:])
        ones = keep.tile([P, P], BF16)
        nc.vector.memset(ones[:], 1.0)

        masked = keep.tile([P, W_TILES, SIZE_IN], BF16)
        x_grouped = keep.tile([P, X_TILES, PASSES, K_PASS], BF16, align_bytes=64)
        w_grouped = keep.tile([P, W_TILES, PASSES, K_PASS], BF16, align_bytes=64)
        x_codes = keep.tile([P, X_TILES, PASSES, P], U32, align_bytes=64)
        x_scales = keep.tile([P, X_TILES, PASSES, P], U8, align_bytes=64)
        w_codes = keep.tile([P, W_TILES, PASSES, P], U32, align_bytes=64)
        w_scales = keep.tile([P, W_TILES, PASSES, P], U8, align_bytes=64)
        bias_all = keep.tile([P, SIZE_OUT], F32)
        result = keep.tile([P, X_TILES, SIZE_OUT], F32)
        out_view = out.rearrange("(p t) n -> p t n", t=X_TILES)

        def flip(rows, grouped, last_parts=1):
            words = rows.bitcast(F32)
            for g in range(PASSES):
                flipped = flip_banks.tile([P, PAIRS, P], F32, tag="flipped")
                for u in range(PAIRS):
                    block = PAIRS * g + u
                    nc.tensor.transpose(flipped[:, u, :], words[:, block * P : (block + 1) * P], identity[:])
                words_out = grouped[:, g, :].bitcast(F32).rearrange("p (r u) -> p r u", u=PAIRS)
                words_in = flipped[:].rearrange("p u r -> p r u")
                parts = last_parts if g == PASSES - 1 else 1
                for h in range(parts):
                    r = slice(h * P // parts, (h + 1) * P // parts)
                    nc.scalar.copy(out=words_out[:, r, :], in_=words_in[:, r, :])

        def quantise(grouped, codes, scales):
            for g in range(PASSES):
                nc.vector.quantize_mx(
                    out=codes[:, g, :].bitcast(FP8X4), scales=scales[:, g, :], in_=grouped[:, g, :]
                )

        def apply_mask(j):
            block = K_PASS // PAIRS
            bounds = [0, K_PASS, SIZE_IN] if j < W_TILES - 1 else [0, K_PASS, K_PASS + block, SIZE_IN]
            for first, end in zip(bounds[:-1], bounds[1:]):
                k_cols = slice(first, end)
                nc.vector.tensor_tensor(
                    out=masked[:, j, k_cols], in0=w_rows[:, j, k_cols], in1=m_rows[:, j, k_cols],
                    op=mybir.AluOpType.mult,
                )

        def multiply_pass(out, j, t, g):
            nc.tensor.matmul_mx(
                out=out,
                lhsT=x_codes[:, t, g, :].bitcast(FP8X4),
                lhsT_scale=x_scales[:, t, g, :],
                rhs=w_codes[:, j, g, :].bitcast(FP8X4),
                rhs_scale=w_scales[:, j, g, :],
                start=(g == 0),
                stop=(g == PASSES - 1),
            )

        def multiply(j):
            sums = sum_banks.tile([P, X_TILES, P], F32)
            for t in range(X_TILES):
                for g in range(PASSES):
                    multiply_pass(sums[:, t, :], j, t, g)
            return sums

        def add_bias_and_store(j, sums):
            n_cols = slice(j * P, (j + 1) * P)
            nc.vector.tensor_tensor(
                out=result[:, :, n_cols],
                in0=sums[:],
                in1=bias_all[:, n_cols].unsqueeze(1).to_broadcast([P, X_TILES, P]),
                op=mybir.AluOpType.add,
            )
            nc.sync.dma_start(out=out_view[:, :, n_cols], in_=result[:, :, n_cols])

        for t in range(X_TILES):
            flip(x_rows[:, t, :], x_grouped[:, t, :, :])
        apply_mask(0)
        for t in range(X_TILES):
            quantise(x_grouped[:, t, :, :], x_codes[:, t, :, :], x_scales[:, t, :, :])
        flip(masked[:, 0, :], w_grouped[:, 0, :, :])

        bias_bank = flip_banks.tile([P, SIZE_OUT], F32, tag="flipped")
        nc.tensor.matmul(bias_bank[:], lhsT=ones[:], rhs=bias_rows[:], start=True, stop=True)
        nc.scalar.copy(out=bias_all[:], in_=bias_bank[:])

        apply_mask(1)
        flip(masked[:, 1, :], w_grouped[:, 1, :, :])

        sums = {}
        quantise(w_grouped[:, 0, :, :], w_codes[:, 0, :, :], w_scales[:, 0, :, :])
        sums[0] = multiply(0)
        last = W_TILES - 1
        for j in range(2, last):
            apply_mask(j)
            flip(masked[:, j, :], w_grouped[:, j, :, :])
        apply_mask(last)
        flip(masked[:, last, :], w_grouped[:, last, :, :], last_parts=HALVES)
        add_bias_and_store(0, sums[0])

        for j in range(1, last):
            quantise(w_grouped[:, j, :, :], w_codes[:, j, :, :], w_scales[:, j, :, :])
            sums[j] = multiply(j)

        halves = [sum_banks.tile([P, X_TILES, P], F32, name=f"half{t}", tag="sums") for t in range(X_TILES)]
        for g in range(PASSES):
            parts = HALVES if g == PASSES - 1 else 1
            for h in range(parts):
                r = slice(h * P // parts, (h + 1) * P // parts)
                k_values = slice(h * K_PASS // parts, (h + 1) * K_PASS // parts)
                nc.vector.quantize_mx(
                    out=w_codes[:, last, g, r].bitcast(FP8X4),
                    scales=w_scales[:, last, g, r],
                    in_=w_grouped[:, last, g, k_values],
                )
            for t in range(X_TILES):
                multiply_pass(halves[t][:, 0, :], last, t, g)
        for j in range(1, last):
            add_bias_and_store(j, sums[j])
        n_cols = slice(last * P, W_TILES * P)
        for t in range(X_TILES):
            nc.vector.tensor_tensor(
                out=result[:, t, n_cols], in0=halves[t][:, 0, :], in1=bias_all[:, n_cols], op=mybir.AluOpType.add
            )
        nc.sync.dma_start(out=out_view[:, :, n_cols], in_=result[:, :, n_cols])
